import numpy as np
import ml_dtypes


def mxq(x, axis, fmt="e4m3"):
    dtype, down = {"e4m3": (ml_dtypes.float8_e4m3fn, 7), "e5m2": (ml_dtypes.float8_e5m2, 14)}[fmt]
    v = np.moveaxis(np.asarray(x, np.float32).astype(ml_dtypes.bfloat16).astype(np.float64), axis, -1)
    blocks = v.reshape(v.shape[:-1] + (-1, 32))
    amax = np.abs(blocks).max(-1, keepdims=True)
    byte = np.maximum(np.where(amax > 0, np.frexp(amax)[1] - 1 + 127, 0) - down, 1)
    scale = np.exp2(byte - 127.0)
    codes = (blocks / scale).astype(np.float32).astype(dtype).astype(np.float64)
    return np.moveaxis((codes * scale).reshape(v.shape), -1, axis)


WIDE = False


def mx_kscale(k):
    if not WIDE:
        return np.ones(k)
    levels = np.array([18, -18])
    if k % 512:
        return np.exp2(np.random.permutation(np.resize(levels, k // 32))).repeat(32)
    a = np.empty((k // 512, 16))
    for p in range(k // 512):
        a[p, :8] = np.random.permutation(np.resize(levels, 8))
        for g in range(8):
            far = levels[np.abs(levels - a[p, g]) >= 10]
            a[p, g + 8] = far[np.random.randint(len(far))]
    return np.exp2(a.ravel()).repeat(32)


BF16 = ml_dtypes.bfloat16


def bf(x):
    return np.asarray(x, np.float32).astype(BF16)


def f64(x):
    return np.asarray(x).astype(np.float64)


N, DIN, DOUT, E, K, B = 512, 8, 64, 16, 3, 64
C = DIN + DOUT
ES = 2.8 / np.sqrt(E)


def sigmoid(v):
    return 1.0 / (1.0 + np.exp(-v))


def draw_adj():
    g = np.random.standard_normal((N, N))
    l = ES**2 * np.sqrt(E) * (g + g.T) / np.sqrt(2.0)
    idx = np.arange(N)
    l[idx, idx] = ES**2 * (E + np.sqrt(2.0 * E) * np.random.standard_normal(N))
    l = np.maximum(l, 0.0)
    e = np.exp(l - l.max(1, keepdims=True))
    return e / e.sum(1, keepdims=True)


def setup_inputs():
    s = mx_kscale(2 * N).reshape(2, N)
    u = mx_kscale(B * C).reshape(B, C)
    adj = draw_adj()
    cheb2 = 2.0 * draw_adj() - np.eye(N)
    adj = bf(f64(bf(adj)) / s[0][:, None])
    cheb2 = bf(f64(bf(cheb2)) / s[1][:, None])
    x = bf(np.random.standard_normal((B, N, DIN)) * u[:, None, :DIN])
    state = bf(np.random.standard_normal((B, N, DOUT)) * u[:, None, DIN:])
    r_logit = bf(np.random.standard_normal((B, N, DOUT)) * 0.8)
    g = np.random.standard_normal((B, N, 2, C)) * np.exp2(np.random.randint(-6, 1, (B, N, 1, 1))) * 2.0
    g = bf(g * s.T[None, :, :, None] / u[:, None, None, :])
    return {"adj": adj, "cheb2": cheb2, "x": x, "state": state, "r_logit": r_logit, "grad_out": g}


def reference(adj, cheb2, x, state, r_logit, grad_out):
    g = f64(grad_out)
    r = sigmoid(f64(r_logit))
    a = np.concatenate([f64(adj), f64(cheb2)], axis=0)
    gs = g[:, :, :, DIN:].transpose(2, 1, 0, 3).reshape(2 * N, B * DOUT)
    ds = mxq(a, 0, "e4m3").T @ mxq(gs, 0, "e5m2")
    dstate = r * ds.reshape(N, B, DOUT).transpose(1, 0, 2)
    cand = np.concatenate([f64(x), r * f64(state)], axis=-1)
    ck = cand.transpose(1, 0, 2).reshape(N, B * C)
    g1 = g[:, :, 0, :].transpose(1, 0, 2).reshape(N, B * C)
    dadj = mxq(g1, 1, "e5m2") @ mxq(ck, 1, "e4m3").T
    return dstate, dadj

@@ -1,0 +1,251 @@
+from contextlib import ExitStack
+
+import concourse.mybir as mybir
+from concourse.masks import make_identity
+
+N, DIN, DOUT, B = 512, 8, 64, 64
+C = DIN + DOUT
+
+FLOPS = 2 * (2 * N) * N * (B * DOUT) + 2 * N * N * (B * C)
+BYTES = 2 * (2 * N * N + B * N * DIN + 2 * B * N * DOUT + B * N * (C + DOUT)) + 4 * (B * N * DOUT + N * N)
+
+F32 = mybir.dt.float32
+BF16 = mybir.dt.bfloat16
+U32 = mybir.dt.uint32
+U8 = mybir.dt.uint8
+E4M3 = mybir.dt.float8_e4m3fn_x4
+E5M2 = mybir.dt.float8_e5m2_x4
+SIGMOID = mybir.ActivationFunctionType.Sigmoid
+MULT = mybir.AluOpType.mult
+
+P = 128
+J = 4
+CB = 8
+CHUNKS = B // CB
+KP = P * J
+WORDS = KP // 2
+CW = C // 2
+XW = DIN // 2
+
+
+def tile_agcrnlayer_pb_v_kernel(tc, adj, cheb2, x, state, r_logit, grad_out, out_0, out_1):
+    nc = tc.nc
+    with ExitStack() as ctx:
+        keep = ctx.enter_context(tc.tile_pool(name="keep", bufs=1))
+        load = ctx.enter_context(tc.tile_pool(name="load", bufs=3))
+        work = ctx.enter_context(tc.tile_pool(name="work", bufs=2))
+        outp = ctx.enter_context(tc.tile_pool(name="outp", bufs=4))
+        ps_acc = ctx.enter_context(tc.psum_pool(name="ps_acc", bufs=1))
+        ps_rot = ctx.enter_context(tc.psum_pool(name="ps_rot", bufs=2))
+        ctx.enter_context(tc.manual_schedule())
+
+        ident = keep.tile([P, P], F32, name="ident")
+        make_identity(nc, ident[:])
+
+        acc = [ps_acc.tile([P, N], F32, name="acc%d" % j, tag="acc%d" % j) for j in range(J)]
+        left_g = keep.tile([P, J, KP], BF16, name="left_g")
+        left_c = keep.tile([P, J, KP], BF16, name="left_c")
+
+        raw = {}
+        gate = {}
+        grouped_g = {}
+        codes_g = {}
+        rows = {}
+        turned = {}
+        codes_t = {}
+        sums = {}
+        result = {}
+
+        def load_logit(c):
+            t = load.tile([P, CB, J * DOUT], BF16, name="logit", tag="logit")
+            nc.sync.dma_start(out=t[:], in_=r_logit[c * CB:(c + 1) * CB].rearrange("b (p j) c -> p b (j c)", j=J))
+            raw[c, "logit"] = t
+
+        def load_rest(c):
+            bs = slice(c * CB, (c + 1) * CB)
+            t = load.tile([P, CB, J * 2 * C], BF16, name="grad", tag="grad")
+            nc.sync.dma_start(out=t[:], in_=grad_out[bs].rearrange("b (p j) o c -> p b (j o c)", j=J))
+            raw[c, "grad"] = t
+            t = load.tile([P, CB, J * DOUT], BF16, name="stat", tag="stat")
+            nc.sync.dma_start(out=t[:], in_=state[bs].rearrange("b (p j) c -> p b (j c)", j=J))
+            raw[c, "state"] = t
+            t = load.tile([P, CB, J * DIN], BF16, name="xin", tag="xin")
+            nc.sync.dma_start(out=t[:], in_=x[bs].rearrange("b (p j) c -> p b (j c)", j=J))
+            raw[c, "x"] = t
+
+        def quantize(src, name, fmt, pool):
+            codes = pool.tile([P, KP], U32, name=name + "_codes", tag=name + "_codes", align_bytes=64)
+            scales = pool.tile([P, KP], U8, name=name + "_scales", tag=name + "_scales", align_bytes=64)
+            nc.vector.quantize_mx(out=codes[:].bitcast(fmt), scales=scales[:], in_=src[:])
+            return codes, scales
+
+        def sigmoid(c):
+            t = load.tile([P, CB, J * DOUT], F32, name="gate", tag="gate")
+            nc.scalar.activation(out=t[:], in_=raw[c, "logit"][:], func=SIGMOID)
+            gate[c] = t
+
+        def interleave_grad(c, o):
+            t = work.tile([P, CB * DOUT * J], BF16, name="gil%d" % o, tag="gil%d" % o, align_bytes=64)
+            src = raw[c, "grad"][:].rearrange("p b (j o c) -> p b j o c", j=J, o=2)[:, :, :, o, DIN:C]
+            src = src.rearrange("p b j (q i) -> p b q j i", i=4)
+            dst = t[:].rearrange("p (b q i j) -> p b q j i", b=CB, i=4, j=J)
+            if o == 0:
+                nc.vector.tensor_copy(out=dst, in_=src)
+            else:
+                nc.scalar.copy(out=dst, in_=src)
+            grouped_g[c, o] = t
+
+        def quantize_grad(c, o):
+            codes_g[c, o] = quantize(grouped_g[c, o], "g%d" % o, E5M2, work)
+
+        def compact_grad(c):
+            t = work.tile([P, J, CB * C], BF16, name="rows_g", tag="rows_g")
+            words = raw[c, "grad"][:].bitcast(F32).rearrange("p b (j w) -> p b j w", j=J)
+            nc.scalar.copy(out=t[:].bitcast(F32).rearrange("p j (b w) -> p b j w", b=CB), in_=words[:, :, :, 0:CW])
+            lw = DOUT // 2
+            nc.scalar.copy(out=left_g[:].bitcast(F32)[:, :, c * lw:(c + 1) * lw], in_=words[:, CB - 1, :, XW:CW])
+            rows[c, "g"] = t
+
+        def build_cand(c):
+            t = work.tile([P, J, CB * C], BF16, name="rows_c", tag="rows_c")
+            view = t[:].rearrange("p j (b c) -> p b j c", b=CB)
+            nc.vector.tensor_copy(out=view[:, :, :, 0:DIN], in_=raw[c, "x"][:].rearrange("p b (j c) -> p b j c", j=J))
+            r = gate[c][:].rearrange("p b (j c) -> p b j c", j=J)
+            s = raw[c, "state"][:].rearrange("p b (j c) -> p b j c", j=J)
+            nc.vector.tensor_tensor(out=view[:, 0:CB - 1, :, DIN:C], in0=r[:, 0:CB - 1], in1=s[:, 0:CB - 1], op=MULT)
+            nc.vector.tensor_tensor(out=left_c[:, :, c * DOUT:(c + 1) * DOUT], in0=r[:, CB - 1], in1=s[:, CB - 1], op=MULT)
+            rows[c, "c"] = t
+
+        def transpose_rows(g, which):
+            words = rows[g, which][:].bitcast(F32)
+            banks = []
+            for h in range(2):
+                bank = ps_rot.tile([P, 2, 2, P], F32, name="bank_t", tag="bank_t")
+                for jj in range(2):
+                    for u in range(2):
+                        nc.tensor.transpose(bank[:, jj, u, :], words[:, 2 * h + jj, u:WORDS:2], ident[:])
+                banks.append(bank)
+            turned[g, which, "banks"] = banks
+
+        def empty_transposed(g, which):
+            t = work.tile([P, N * J], BF16, name="turned_" + which, tag="turned_" + which, align_bytes=64)
+            view = t[:].bitcast(F32).rearrange("q (j r u) -> q j r u", j=J, u=2)
+            for h in range(2):
+                nc.scalar.copy(out=view[:, 2 * h:2 * h + 2], in_=turned[g, which, "banks"][h][:].rearrange("q j u r -> q j r u"))
+            turned[g, which] = t
+
+        def quantize_turned(g, which):
+            codes_t[g, which] = quantize(turned[g, which], "t" + which, E5M2 if which == "g" else E4M3, work)
+
+        def state_product(c, t):
+            bank = ps_rot.tile([P, KP], F32, name="bank_s", tag="bank_s")
+            cols = slice(t * P, (t + 1) * P)
+            for o in range(2):
+                a_codes, a_scales = codes_a[o]
+                g_codes, g_scales = codes_g[c, o]
+                nc.tensor.matmul_mx(out=bank[:], lhsT=a_codes[:, cols].bitcast(E4M3), lhsT_scale=a_scales[:, cols],
+                                    rhs=g_codes[:].bitcast(E5M2), rhs_scale=g_scales[:], start=(o == 0), stop=(o == 1))
+            sums[c, t] = bank
+
+        def gate_and_empty(c, t):
+            if t == 0:
+                result[c] = outp.tile([P, CB, J * DOUT], F32, name="dstate", tag="dstate")
+            cols = slice(t * DOUT, (t + 1) * DOUT)
+            nc.vector.tensor_tensor(out=result[c][:, :, cols], in0=sums[c, t][:].rearrange("p (b c) -> p b c", b=CB),
+                                    in1=gate[c][:, :, cols], op=MULT)
+
+        def store_state(c):
+            nc.sync.dma_start(out=out_0[c * CB:(c + 1) * CB].rearrange("b (p j) c -> p b (j c)", j=J), in_=result[c][:])
+
+        def adj_product(g, j):
+            g_codes, g_scales = codes_t[g, "g"]
+            c_codes, c_scales = codes_t[g, "c"]
+            cols = slice(j * P, (j + 1) * P)
+            nc.tensor.matmul_mx(out=acc[j][:], lhsT=g_codes[:, cols].bitcast(E5M2), lhsT_scale=g_scales[:, cols],
+                                rhs=c_codes[:].bitcast(E4M3), rhs_scale=c_scales[:], start=(g == 0), stop=(g == CHUNKS))
+
+        load_logit(0)
+        a_raw = []
+        for o, a in enumerate((adj, cheb2)):
+            t = keep.tile([P, J, N], BF16, name="a_raw%d" % o)
+            nc.sync.dma_start(out=t[:], in_=a.rearrange("(p j) n -> p j n", j=J))
+            a_raw.append(t)
+        load_rest(0)
+        load_logit(1)
+        load_rest(1)
+        a_grouped = []
+        for o in range(2):
+            t = keep.tile([P, N * J], BF16, name="a_grouped%d" % o, align_bytes=64)
+            nc.vector.tensor_copy(out=t[:].rearrange("p (t m j) -> p t m j", t=J, j=J),
+                                  in_=a_raw[o][:].rearrange("p j (m t) -> p t m j", t=J))
+            a_grouped.append(t)
+        codes_a = [quantize(a_grouped[o], "a%d" % o, E4M3, keep) for o in range(2)]
+
+        rows[CHUNKS, "g"] = left_g
+        rows[CHUNKS, "c"] = left_c
+
+        for s in range(CHUNKS + 1):
+            new = s < CHUNKS
+            old = s - 1
+            if s + 2 < CHUNKS:
+                load_logit(s + 2)
+                load_rest(s + 2)
+            if new:
+                sigmoid(s)
+            if old >= 0:
+                quantize_grad(old, 0)
+                quantize_grad(old, 1)
+                transpose_rows(old, "g")
+                state_product(old, 0)
+                state_product(old, 1)
+            if new:
+                interleave_grad(s, 0)
+            if old >= 0:
+                empty_transposed(old, "g")
+            if old >= 1:
+                for j in range(J):
+                    adj_product(old - 1, j)
+            if old >= 0:
+                gate_and_empty(old, 0)
+                gate_and_empty(old, 1)
+                transpose_rows(old, "c")
+                state_product(old, 2)
+                state_product(old, 3)
+            if new:
+                interleave_grad(s, 1)
+                build_cand(s)
+            if old >= 0:
+                empty_transposed(old, "c")
+                gate_and_empty(old, 2)
+                gate_and_empty(old, 3)
+                store_state(old)
+            if not new:
+                transpose_rows(CHUNKS, "g")
+                empty_transposed(CHUNKS, "g")
+            if old >= 0:
+                quantize_turned(old, "g")
+                quantize_turned(old, "c")
+            if new:
+                compact_grad(s)
+
+        last = CHUNKS
+        transpose_rows(last, "c")
+        empty_transposed(last, "c")
+        for j in range(J):
+            adj_product(last - 1, j)
+        quantize_turned(last, "g")
+        quantize_turned(last, "c")
+        out_rows = out_1.rearrange("(p j) n -> p j n", j=J)
+        for j in range(J):
+            adj_product(last, j)
+        for h in range(2):
+            t = keep.tile([P, 2, N], F32, name="dadj%d" % h)
+            for jj in range(2):
+                j = 2 * h + jj
+                dst = t[:, jj, :].rearrange("p (r i) -> p r i", i=J)
+                src = acc[j][:].rearrange("p (i r) -> p r i", i=J)
+                if jj == 0:
+                    nc.vector.tensor_copy(out=dst, in_=src)
+                else:
+                    nc.scalar.copy(out=dst, in_=src)
+            nc.sync.dma_start(out=out_rows[:, 2 * h:2 * h + 2, :], in_=t[:])

@@ -46,7 +46,11 @@ def tile_agcrnlayer_pb_v_kernel(tc, adj, cheb2, x, state, r_logit, grad_out, out
         left_g = keep.tile([P, J, KP], BF16, name="left_g")
         left_c = keep.tile([P, J, KP], BF16, name="left_c")
 
+        x_rows = keep.tile([P, N * DIN], BF16, name="x_rows")
+        x_nodes = keep.tile([P, B, J * DIN], BF16, name="x_nodes")
+
         raw = {}
+        codes_a = {}
         gate = {}
         grouped_g = {}
         codes_g = {}
@@ -69,9 +73,35 @@ def tile_agcrnlayer_pb_v_kernel(tc, adj, cheb2, x, state, r_logit, grad_out, out
             t = load.tile([P, CB, J * DOUT], BF16, name="stat", tag="stat")
             nc.sync.dma_start(out=t[:], in_=state[bs].rearrange("b (p j) c -> p b (j c)", j=J))
             raw[c, "state"] = t
-            t = load.tile([P, CB, J * DIN], BF16, name="xin", tag="xin")
-            nc.sync.dma_start(out=t[:], in_=x[bs].rearrange("b (p j) c -> p b (j c)", j=J))
-            raw[c, "x"] = t
+
+        def load_adj(o):
+            t = keep.tile([P, J, N], BF16, name="a_raw%d" % o)
+            nc.sync.dma_start(out=t[:], in_=(adj, cheb2)[o].rearrange("(p j) n -> p j n", j=J))
+            raw["a", o] = t
+
+        def interleave_adj(o):
+            t = keep.tile([P, N * J], BF16, name="a_grouped%d" % o, align_bytes=64)
+            nc.vector.tensor_copy(out=t[:].rearrange("p (t m j) -> p t m j", t=J, j=J),
+                                  in_=raw["a", o][:].rearrange("p j (m t) -> p t m j", t=J))
+            grouped_g["a", o] = t
+
+        def quantize_adj(o):
+            codes_a[o] = quantize(grouped_g["a", o], "a%d" % o, E4M3, keep)
+
+        def load_x():
+            flat = x.rearrange("b n c -> b (n c)")
+            nc.sync.dma_start(out=x_rows[0:B, :], in_=flat)
+            nc.sync.dma_start(out=x_rows[B:P, 0:(N - 2) * DIN], in_=flat[:, 2 * DIN:N * DIN])
+
+        def turn_x():
+            words = x_rows[:].bitcast(F32)
+            dst = x_nodes[:].bitcast(F32).rearrange("p b (h l w) -> p h l b w", h=2, l=2)
+            for l in range(2):
+                bank = ps_rot.tile([P, XW, P], F32, name="bank_t", tag="bank_t")
+                for w in range(XW):
+                    first = l * XW + w
+                    nc.tensor.transpose(bank[:, w, :], words[:, first:first + (P - 1) * J * XW + 1:J * XW], ident[:])
+                nc.scalar.copy(out=dst[:, :, l], in_=bank[:].rearrange("p w (h b) -> p h b w", h=2))
 
         def quantize(src, name, fmt, pool):
             codes = pool.tile([P, KP], U32, name=name + "_codes", tag=name + "_codes", align_bytes=64)
@@ -109,12 +139,16 @@ def tile_agcrnlayer_pb_v_kernel(tc, adj, cheb2, x, state, r_logit, grad_out, out
         def build_cand(c):
             t = work.tile([P, J, CB * C], BF16, name="rows_c", tag="rows_c")
             view = t[:].rearrange("p j (b c) -> p b j c", b=CB)
-            nc.vector.tensor_copy(out=view[:, :, :, 0:DIN], in_=raw[c, "x"][:].rearrange("p b (j c) -> p b j c", j=J))
             r = gate[c][:].rearrange("p b (j c) -> p b j c", j=J)
             s = raw[c, "state"][:].rearrange("p b (j c) -> p b j c", j=J)
             nc.vector.tensor_tensor(out=view[:, 0:CB - 1, :, DIN:C], in0=r[:, 0:CB - 1], in1=s[:, 0:CB - 1], op=MULT)
             nc.vector.tensor_tensor(out=left_c[:, :, c * DOUT:(c + 1) * DOUT], in0=r[:, CB - 1], in1=s[:, CB - 1], op=MULT)
             rows[c, "c"] = t
+
+        def copy_x(c):
+            view = rows[c, "c"][:].rearrange("p j (b c) -> p b j c", b=CB)
+            nc.vector.tensor_copy(out=view[:, :, :, 0:DIN],
+                                  in_=x_nodes[:, c * CB:(c + 1) * CB, :].rearrange("p b (j c) -> p b j c", j=J))
 
         def transpose_rows(g, which):
             words = rows[g, which][:].bitcast(F32)
@@ -164,88 +198,131 @@ def tile_agcrnlayer_pb_v_kernel(tc, adj, cheb2, x, state, r_logit, grad_out, out
             nc.tensor.matmul_mx(out=acc[j][:], lhsT=g_codes[:, cols].bitcast(E5M2), lhsT_scale=g_scales[:, cols],
                                 rhs=c_codes[:].bitcast(E4M3), rhs_scale=c_scales[:], start=(g == 0), stop=(g == CHUNKS))
 
-        load_logit(0)
-        a_raw = []
-        for o, a in enumerate((adj, cheb2)):
-            t = keep.tile([P, J, N], BF16, name="a_raw%d" % o)
-            nc.sync.dma_start(out=t[:], in_=a.rearrange("(p j) n -> p j n", j=J))
-            a_raw.append(t)
-        load_rest(0)
-        load_logit(1)
-        load_rest(1)
-        a_grouped = []
-        for o in range(2):
-            t = keep.tile([P, N * J], BF16, name="a_grouped%d" % o, align_bytes=64)
-            nc.vector.tensor_copy(out=t[:].rearrange("p (t m j) -> p t m j", t=J, j=J),
-                                  in_=a_raw[o][:].rearrange("p j (m t) -> p t m j", t=J))
-            a_grouped.append(t)
-        codes_a = [quantize(a_grouped[o], "a%d" % o, E4M3, keep) for o in range(2)]
+        def load_chunk(c):
+            load_logit(c)
+            load_rest(c)
 
         rows[CHUNKS, "g"] = left_g
         rows[CHUNKS, "c"] = left_c
 
-        for s in range(CHUNKS + 1):
-            new = s < CHUNKS
+        load_adj(0)
+        load_logit(0)
+        load_rest(0)
+        load_x()
+        load_adj(1)
+        load_chunk(1)
+        load_chunk(2)
+        sigmoid(0)
+        interleave_adj(0)
+        quantize_adj(0)
+        interleave_grad(0, 0)
+        interleave_grad(0, 1)
+        compact_grad(0)
+        build_cand(0)
+        quantize_grad(0, 0)
+        quantize_grad(0, 1)
+        turn_x()
+        transpose_rows(0, "g")
+        interleave_adj(1)
+        copy_x(0)
+        quantize_adj(1)
+
+        load_chunk(3)
+        sigmoid(1)
+        state_product(0, 0)
+        state_product(0, 1)
+        empty_transposed(0, "g")
+        transpose_rows(0, "c")
+        gate_and_empty(0, 0)
+        gate_and_empty(0, 1)
+        state_product(0, 2)
+        state_product(0, 3)
+        interleave_grad(1, 0)
+        empty_transposed(0, "c")
+        compact_grad(1)
+        gate_and_empty(0, 2)
+        gate_and_empty(0, 3)
+        build_cand(1)
+        copy_x(1)
+        transpose_rows(1, "g")
+        interleave_grad(1, 1)
+        quantize_turned(0, "g")
+        quantize_turned(0, "c")
+        adj_product(0, 0)
+        adj_product(0, 1)
+
+        for s in range(2, CHUNKS):
             old = s - 1
             if s + 2 < CHUNKS:
-                load_logit(s + 2)
-                load_rest(s + 2)
-            if new:
-                sigmoid(s)
-            if old >= 0:
-                quantize_grad(old, 0)
-                quantize_grad(old, 1)
-                transpose_rows(old, "g")
-                state_product(old, 0)
-                state_product(old, 1)
-            if new:
-                interleave_grad(s, 0)
-            if old >= 0:
-                empty_transposed(old, "g")
-            if old >= 1:
-                for j in range(J):
-                    adj_product(old - 1, j)
-            if old >= 0:
-                gate_and_empty(old, 0)
-                gate_and_empty(old, 1)
-                transpose_rows(old, "c")
-                state_product(old, 2)
-                state_product(old, 3)
-            if new:
-                interleave_grad(s, 1)
-                build_cand(s)
-            if old >= 0:
-                empty_transposed(old, "c")
-                gate_and_empty(old, 2)
-                gate_and_empty(old, 3)
+                load_chunk(s + 2)
+            if s + 2 <= CHUNKS:
+                store_state(s - 2)
+            sigmoid(s)
+            quantize_grad(old, 0)
+            quantize_grad(old, 1)
+            state_product(old, 0)
+            state_product(old, 1)
+            empty_transposed(old, "g")
+            interleave_grad(s, 0)
+            transpose_rows(old, "c")
+            adj_product(old - 1, 2)
+            adj_product(old - 1, 3)
+            compact_grad(s)
+            build_cand(s)
+            copy_x(s)
+            empty_transposed(old, "c")
+            gate_and_empty(old, 0)
+            gate_and_empty(old, 1)
+            state_product(old, 2)
+            state_product(old, 3)
+            transpose_rows(s, "g")
+            interleave_grad(s, 1)
+            quantize_turned(old, "g")
+            quantize_turned(old, "c")
+            adj_product(old, 0)
+            adj_product(old, 1)
+            gate_and_empty(old, 2)
+            gate_and_empty(old, 3)
+            if s + 2 >= CHUNKS:
                 store_state(old)
-            if not new:
-                transpose_rows(CHUNKS, "g")
-                empty_transposed(CHUNKS, "g")
-            if old >= 0:
-                quantize_turned(old, "g")
-                quantize_turned(old, "c")
-            if new:
-                compact_grad(s)
 
+        old = CHUNKS - 1
         last = CHUNKS
+        empty_transposed(old, "g")
+        quantize_grad(old, 0)
+        quantize_grad(old, 1)
+        transpose_rows(old, "c")
+        state_product(old, 0)
+        state_product(old, 1)
+        adj_product(old - 1, 2)
+        adj_product(old - 1, 3)
+        quantize_turned(old, "g")
+        empty_transposed(old, "c")
+        gate_and_empty(old, 0)
+        gate_and_empty(old, 1)
+        transpose_rows(last, "g")
+        state_product(old, 2)
+        state_product(old, 3)
+        quantize_turned(old, "c")
+        empty_transposed(last, "g")
+        gate_and_empty(old, 2)
+        gate_and_empty(old, 3)
+        store_state(old)
         transpose_rows(last, "c")
-        empty_transposed(last, "c")
         for j in range(J):
-            adj_product(last - 1, j)
+            adj_product(old, j)
         quantize_turned(last, "g")
+        empty_transposed(last, "c")
         quantize_turned(last, "c")
         out_rows = out_1.rearrange("(p j) n -> p j n", j=J)
         for j in range(J):
             adj_product(last, j)
-        for h in range(2):
-            t = keep.tile([P, 2, N], F32, name="dadj%d" % h)
-            for jj in range(2):
-                j = 2 * h + jj
-                dst = t[:, jj, :].rearrange("p (r i) -> p r i", i=J)
-                src = acc[j][:].rearrange("p (i r) -> p r i", i=J)
-                if jj == 0:
-                    nc.vector.tensor_copy(out=dst, in_=src)
-                else:
-                    nc.scalar.copy(out=dst, in_=src)
-            nc.sync.dma_start(out=out_rows[:, 2 * h:2 * h + 2, :], in_=t[:])
+        for j in range(J):
+            t = keep.tile([P, N], F32, name="dadj%d" % j)
+            dst = t[:].rearrange("p (r i) -> p r i", i=J)
+            src = acc[j][:].rearrange("p (i r) -> p r i", i=J)
+            if j % 2 == 0:
+                nc.scalar.copy(out=dst, in_=src)
+            else:
+                nc.vector.tensor_copy(out=dst, in_=src)
+            nc.sync.dma_start(out=out_rows[:, j, :], in_=t[:])

@@ -20,12 +20,23 @@ MULT = mybir.AluOpType.mult
 
 P = 128
 J = 4
-CB = 8
-CHUNKS = B // CB
+GROUP = 8
+CHUNKS = B // GROUP + 1
 KP = P * J
 WORDS = KP // 2
 CW = C // 2
 XW = DIN // 2
+SW = DOUT // 2
+
+
+def entries(c):
+    if c == 0:
+        return slice(GROUP - 1, B, GROUP)
+    return slice((c - 1) * GROUP, c * GROUP - 1)
+
+
+def width(c):
+    return GROUP if c == 0 else GROUP - 1
 
 
 def tile_agcrnlayer_pb_v_kernel(tc, adj, cheb2, x, state, r_logit, grad_out, out_0, out_1):
@@ -39,20 +50,21 @@ def tile_agcrnlayer_pb_v_kernel(tc, adj, cheb2, x, state, r_logit, grad_out, out
         ps_rot = ctx.enter_context(tc.psum_pool(name="ps_rot", bufs=2))
         ctx.enter_context(tc.manual_schedule())
 
+        on_v = nc.vector.tensor_copy
+        on_s = nc.scalar.copy
+
         ident = keep.tile([P, P], F32, name="ident")
         make_identity(nc, ident[:])
 
         acc = [ps_acc.tile([P, N], F32, name="acc%d" % j, tag="acc%d" % j) for j in range(J)]
-        left_g = keep.tile([P, J, KP], BF16, name="left_g")
-        left_c = keep.tile([P, J, KP], BF16, name="left_c")
-
+        grouped = [[keep.tile([P, KP * J], BF16, name="gil%d%d" % (i, o), align_bytes=64) for o in range(2)] for i in range(2)]
         x_rows = keep.tile([P, N * DIN], BF16, name="x_rows")
         x_nodes = keep.tile([P, B, J * DIN], BF16, name="x_nodes")
+        heads = keep.tile([P, GROUP, J, XW], F32, name="heads")
 
         raw = {}
         codes_a = {}
         gate = {}
-        grouped_g = {}
         codes_g = {}
         rows = {}
         turned = {}
@@ -60,48 +72,36 @@ def tile_agcrnlayer_pb_v_kernel(tc, adj, cheb2, x, state, r_logit, grad_out, out
         sums = {}
         result = {}
 
-        def load_logit(c):
-            t = load.tile([P, CB, J * DOUT], BF16, name="logit", tag="logit")
-            nc.sync.dma_start(out=t[:], in_=r_logit[c * CB:(c + 1) * CB].rearrange("b (p j) c -> p b (j c)", j=J))
-            raw[c, "logit"] = t
+        def load_logit(c, first=0, stop=None):
+            stop = width(c) if stop is None else stop
+            t = load.tile([P, stop - first, J * DOUT], BF16, name="logit", tag="logit")
+            src = r_logit[entries(c)][first:stop]
+            nc.sync.dma_start(out=t[:], in_=src.rearrange("b (p j) c -> p b (j c)", j=J))
+            raw[c, "logit", first] = t
 
-        def load_rest(c):
-            bs = slice(c * CB, (c + 1) * CB)
-            t = load.tile([P, CB, J * 2 * C], BF16, name="grad", tag="grad")
-            nc.sync.dma_start(out=t[:], in_=grad_out[bs].rearrange("b (p j) o c -> p b (j o c)", j=J))
+        def load_grad(c):
+            t = load.tile([P, width(c), J * 2 * C], BF16, name="grad", tag="grad")
+            nc.sync.dma_start(out=t[:], in_=grad_out[entries(c)].rearrange("b (p j) o c -> p b (j o c)", j=J))
             raw[c, "grad"] = t
-            t = load.tile([P, CB, J * DOUT], BF16, name="stat", tag="stat")
-            nc.sync.dma_start(out=t[:], in_=state[bs].rearrange("b (p j) c -> p b (j c)", j=J))
+
+        def load_state(c):
+            t = load.tile([P, width(c), J * DOUT], BF16, name="stat", tag="stat")
+            nc.sync.dma_start(out=t[:], in_=state[entries(c)].rearrange("b (p j) c -> p b (j c)", j=J))
             raw[c, "state"] = t
+
+        def load_chunk(c):
+            load_logit(c)
+            load_grad(c)
+            load_state(c)
 
         def load_adj(o):
             t = keep.tile([P, J, N], BF16, name="a_raw%d" % o)
             nc.sync.dma_start(out=t[:], in_=(adj, cheb2)[o].rearrange("(p j) n -> p j n", j=J))
             raw["a", o] = t
 
-        def interleave_adj(o):
-            t = keep.tile([P, N * J], BF16, name="a_grouped%d" % o, align_bytes=64)
-            nc.vector.tensor_copy(out=t[:].rearrange("p (t m j) -> p t m j", t=J, j=J),
-                                  in_=raw["a", o][:].rearrange("p j (m t) -> p t m j", t=J))
-            grouped_g["a", o] = t
-
-        def quantize_adj(o):
-            codes_a[o] = quantize(grouped_g["a", o], "a%d" % o, E4M3, keep)
-
-        def load_x():
-            flat = x.rearrange("b n c -> b (n c)")
-            nc.sync.dma_start(out=x_rows[0:B, :], in_=flat)
-            nc.sync.dma_start(out=x_rows[B:P, 0:(N - 2) * DIN], in_=flat[:, 2 * DIN:N * DIN])
-
-        def turn_x():
-            words = x_rows[:].bitcast(F32)
-            dst = x_nodes[:].bitcast(F32).rearrange("p b (h l w) -> p h l b w", h=2, l=2)
-            for l in range(2):
-                bank = ps_rot.tile([P, XW, P], F32, name="bank_t", tag="bank_t")
-                for w in range(XW):
-                    first = l * XW + w
-                    nc.tensor.transpose(bank[:, w, :], words[:, first:first + (P - 1) * J * XW + 1:J * XW], ident[:])
-                nc.scalar.copy(out=dst[:, :, l], in_=bank[:].rearrange("p w (h b) -> p h b w", h=2))
+        def load_x(h):
+            skip = 2 * h * DIN
+            nc.sync.dma_start(out=x_rows[h:P:2, 0:N * DIN - skip], in_=x.rearrange("b n c -> b (n c)")[:, skip:N * DIN])
 
         def quantize(src, name, fmt, pool):
             codes = pool.tile([P, KP], U32, name=name + "_codes", tag=name + "_codes", align_bytes=64)
@@ -109,63 +109,80 @@ def tile_agcrnlayer_pb_v_kernel(tc, adj, cheb2, x, state, r_logit, grad_out, out
             nc.vector.quantize_mx(out=codes[:].bitcast(fmt), scales=scales[:], in_=src[:])
             return codes, scales
 
-        def sigmoid(c):
-            t = load.tile([P, CB, J * DOUT], F32, name="gate", tag="gate")
-            nc.scalar.activation(out=t[:], in_=raw[c, "logit"][:], func=SIGMOID)
-            gate[c] = t
+        def interleave_adj(o):
+            nc.vector.tensor_copy(out=grouped[1][o][:].rearrange("p (t m j) -> p t m j", t=J, j=J),
+                                  in_=raw["a", o][:].rearrange("p j (m t) -> p t m j", t=J))
 
-        def interleave_grad(c, o):
-            t = work.tile([P, CB * DOUT * J], BF16, name="gil%d" % o, tag="gil%d" % o, align_bytes=64)
+        def quantize_adj(o):
+            codes_a[o] = quantize(grouped[1][o], "a%d" % o, E4M3, keep)
+
+        def turn_x():
+            words = x_rows[:].bitcast(F32)
+            dst = x_nodes[:].bitcast(F32).rearrange("p b (h l w) -> p l b h w", h=2, l=2)
+            for l in range(2):
+                bank = ps_rot.tile([P, XW, P], F32, name="bank_t", tag="bank_t")
+                for w in range(XW):
+                    first = l * XW + w
+                    nc.tensor.transpose(bank[:, w, :], words[:, first:first + (P - 1) * J * XW + 1:J * XW], ident[:])
+                nc.scalar.copy(out=dst[:, l], in_=bank[:].rearrange("p w (b h) -> p b h w", h=2))
+
+        def sigmoid(c, first=0, stop=None):
+            stop = width(c) if stop is None else stop
+            if first == 0:
+                gate[c] = load.tile([P, width(c), J * DOUT], F32, name="gate", tag="gate")
+            nc.scalar.activation(out=gate[c][:, first:stop, :], in_=raw[c, "logit", first][:], func=SIGMOID)
+
+        def interleave_grad(c, o, copy, first=0, stop=16):
             src = raw[c, "grad"][:].rearrange("p b (j o c) -> p b j o c", j=J, o=2)[:, :, :, o, DIN:C]
-            src = src.rearrange("p b j (q i) -> p b q j i", i=4)
-            dst = t[:].rearrange("p (b q i j) -> p b q j i", b=CB, i=4, j=J)
-            if o == 0:
-                nc.vector.tensor_copy(out=dst, in_=src)
-            else:
-                nc.scalar.copy(out=dst, in_=src)
-            grouped_g[c, o] = t
+            src = src.rearrange("p b j (q i) -> p q b j i", i=4)
+            dst = grouped[c % 2][o][:].rearrange("p (b q i j) -> p q b j i", b=GROUP, i=4, j=J)
+            copy(out=dst[:, first:stop, 0:width(c)], in_=src[:, first:stop])
 
         def quantize_grad(c, o):
-            codes_g[c, o] = quantize(grouped_g[c, o], "g%d" % o, E5M2, work)
+            codes_g[c, o] = quantize(grouped[c % 2][o], "g%d" % o, E5M2, work)
 
         def compact_grad(c):
-            t = work.tile([P, J, CB * C], BF16, name="rows_g", tag="rows_g")
-            words = raw[c, "grad"][:].bitcast(F32).rearrange("p b (j w) -> p b j w", j=J)
-            nc.scalar.copy(out=t[:].bitcast(F32).rearrange("p j (b w) -> p b j w", b=CB), in_=words[:, :, :, 0:CW])
-            lw = DOUT // 2
-            nc.scalar.copy(out=left_g[:].bitcast(F32)[:, :, c * lw:(c + 1) * lw], in_=words[:, CB - 1, :, XW:CW])
+            t = work.tile([P, J, GROUP * C], BF16, name="rows_g", tag="rows_g")
+            dst = t[:].bitcast(F32)
+            src = raw[c, "grad"][:].bitcast(F32).rearrange("p b (j w) -> p b j w", j=J)
+            if c == 0:
+                nc.scalar.copy(out=dst[:, :, 0:WORDS].rearrange("p j (b w) -> p b j w", b=GROUP), in_=src[:, :, :, XW:CW])
+                nc.scalar.copy(out=heads[:], in_=src[:, :, :, 0:XW])
+            else:
+                dst = dst.rearrange("p j (b w) -> p b j w", b=GROUP)
+                nc.scalar.copy(out=dst[:, 0:GROUP - 1], in_=src[:, :, :, 0:CW])
+                nc.scalar.copy(out=dst[:, GROUP - 1, :, 0:XW], in_=heads[:, c - 1])
             rows[c, "g"] = t
 
         def build_cand(c):
-            t = work.tile([P, J, CB * C], BF16, name="rows_c", tag="rows_c")
-            view = t[:].rearrange("p j (b c) -> p b j c", b=CB)
-            r = gate[c][:].rearrange("p b (j c) -> p b j c", j=J)
-            s = raw[c, "state"][:].rearrange("p b (j c) -> p b j c", j=J)
-            nc.vector.tensor_tensor(out=view[:, 0:CB - 1, :, DIN:C], in0=r[:, 0:CB - 1], in1=s[:, 0:CB - 1], op=MULT)
-            nc.vector.tensor_tensor(out=left_c[:, :, c * DOUT:(c + 1) * DOUT], in0=r[:, CB - 1], in1=s[:, CB - 1], op=MULT)
+            t = work.tile([P, J, GROUP * C], BF16, name="rows_c", tag="rows_c")
+            if c == 0:
+                dst = t[:, :, 0:KP].rearrange("p j (b c) -> p b j c", b=GROUP)
+            else:
+                dst = t[:].rearrange("p j (b c) -> p b j c", b=GROUP)[:, 0:GROUP - 1, :, DIN:C]
+            nc.vector.tensor_tensor(out=dst, in0=gate[c][:].rearrange("p b (j c) -> p b j c", j=J),
+                                    in1=raw[c, "state"][:].rearrange("p b (j c) -> p b j c", j=J), op=MULT)
             rows[c, "c"] = t
 
-        def copy_x(c):
-            view = rows[c, "c"][:].rearrange("p j (b c) -> p b j c", b=CB)
-            nc.vector.tensor_copy(out=view[:, :, :, 0:DIN],
-                                  in_=x_nodes[:, c * CB:(c + 1) * CB, :].rearrange("p b (j c) -> p b j c", j=J))
+        def copy_x(c, copy):
+            view = rows[c, "c"][:].rearrange("p j (b c) -> p b j c", b=GROUP)
+            copy(out=view[:, :, :, 0:DIN],
+                 in_=x_nodes[:, (c - 1) * GROUP:c * GROUP, :].rearrange("p b (j c) -> p b j c", j=J))
 
-        def transpose_rows(g, which):
+        def transpose_rows(g, which, halves=(0, 1)):
             words = rows[g, which][:].bitcast(F32)
-            banks = []
-            for h in range(2):
+            for h in halves:
                 bank = ps_rot.tile([P, 2, 2, P], F32, name="bank_t", tag="bank_t")
                 for jj in range(2):
                     for u in range(2):
                         nc.tensor.transpose(bank[:, jj, u, :], words[:, 2 * h + jj, u:WORDS:2], ident[:])
-                banks.append(bank)
-            turned[g, which, "banks"] = banks
+                turned[g, which, h] = bank
 
-        def empty_transposed(g, which):
+        def empty_transposed(g, which, copies=(on_s, on_s)):
             t = work.tile([P, N * J], BF16, name="turned_" + which, tag="turned_" + which, align_bytes=64)
             view = t[:].bitcast(F32).rearrange("q (j r u) -> q j r u", j=J, u=2)
             for h in range(2):
-                nc.scalar.copy(out=view[:, 2 * h:2 * h + 2], in_=turned[g, which, "banks"][h][:].rearrange("q j u r -> q j r u"))
+                copies[h](out=view[:, 2 * h:2 * h + 2], in_=turned[g, which, h][:].rearrange("q j u r -> q j r u"))
             turned[g, which] = t
 
         def quantize_turned(g, which):
@@ -183,146 +200,166 @@ def tile_agcrnlayer_pb_v_kernel(tc, adj, cheb2, x, state, r_logit, grad_out, out
 
         def gate_and_empty(c, t):
             if t == 0:
-                result[c] = outp.tile([P, CB, J * DOUT], F32, name="dstate", tag="dstate")
+                result[c] = outp.tile([P, width(c), J * DOUT], F32, name="dstate", tag="dstate")
             cols = slice(t * DOUT, (t + 1) * DOUT)
-            nc.vector.tensor_tensor(out=result[c][:, :, cols], in0=sums[c, t][:].rearrange("p (b c) -> p b c", b=CB),
-                                    in1=gate[c][:, :, cols], op=MULT)
+            src = sums[c, t][:].rearrange("p (b c) -> p b c", b=GROUP)[:, 0:width(c)]
+            nc.vector.tensor_tensor(out=result[c][:, :, cols], in0=src, in1=gate[c][:, :, cols], op=MULT)
 
-        def store_state(c):
-            nc.sync.dma_start(out=out_0[c * CB:(c + 1) * CB].rearrange("b (p j) c -> p b (j c)", j=J), in_=result[c][:])
+        def store_state(c, first=0, stop=J):
+            cols = slice(first * DOUT, stop * DOUT)
+            dst = out_0[entries(c)].rearrange("b (p j) c -> p b (j c)", j=J)
+            nc.sync.dma_start(out=dst[:, :, cols], in_=result[c][:, :, cols])
 
         def adj_product(g, j):
             g_codes, g_scales = codes_t[g, "g"]
             c_codes, c_scales = codes_t[g, "c"]
             cols = slice(j * P, (j + 1) * P)
             nc.tensor.matmul_mx(out=acc[j][:], lhsT=g_codes[:, cols].bitcast(E5M2), lhsT_scale=g_scales[:, cols],
-                                rhs=c_codes[:].bitcast(E4M3), rhs_scale=c_scales[:], start=(g == 0), stop=(g == CHUNKS))
+                                rhs=c_codes[:].bitcast(E4M3), rhs_scale=c_scales[:], start=(g == 0), stop=(g == CHUNKS - 1))
 
-        def load_chunk(c):
-            load_logit(c)
-            load_rest(c)
+        def store_adj(j, copy):
+            t = keep.tile([P, N], F32, name="dadj%d" % j)
+            copy(out=t[:].rearrange("p (r i) -> p r i", i=J), in_=acc[j][:].rearrange("p (i r) -> p r i", i=J))
+            nc.sync.dma_start(out=out_1.rearrange("(p j) n -> p j n", j=J)[:, j, :], in_=t[:])
 
-        rows[CHUNKS, "g"] = left_g
-        rows[CHUNKS, "c"] = left_c
-
+        load_logit(0, 0, 1)
         load_adj(0)
-        load_logit(0)
-        load_rest(0)
-        load_x()
         load_adj(1)
-        load_chunk(1)
+        load_grad(0)
+        load_logit(0, 1)
+        load_state(0)
+        load_x(0)
+        load_logit(1)
+        load_x(1)
+        load_grad(1)
+        load_state(1)
+        sigmoid(0, 0, 1)
         load_chunk(2)
-        sigmoid(0)
         interleave_adj(0)
+        interleave_adj(1)
         quantize_adj(0)
-        interleave_grad(0, 0)
-        interleave_grad(0, 1)
+        quantize_adj(1)
         compact_grad(0)
-        build_cand(0)
+        interleave_grad(0, 0, on_v)
+        interleave_grad(0, 1, on_v)
+        transpose_rows(0, "g")
+        sigmoid(0, 1)
         quantize_grad(0, 0)
         quantize_grad(0, 1)
-        turn_x()
-        transpose_rows(0, "g")
-        interleave_adj(1)
-        copy_x(0)
-        quantize_adj(1)
-
-        load_chunk(3)
-        sigmoid(1)
         state_product(0, 0)
         state_product(0, 1)
         empty_transposed(0, "g")
+        build_cand(0)
         transpose_rows(0, "c")
+        load_chunk(3)
+        sigmoid(1)
         gate_and_empty(0, 0)
         gate_and_empty(0, 1)
         state_product(0, 2)
         state_product(0, 3)
-        interleave_grad(1, 0)
+        quantize_turned(0, "g")
         empty_transposed(0, "c")
         compact_grad(1)
+        turn_x()
         gate_and_empty(0, 2)
         gate_and_empty(0, 3)
-        build_cand(1)
-        copy_x(1)
-        transpose_rows(1, "g")
-        interleave_grad(1, 1)
-        quantize_turned(0, "g")
         quantize_turned(0, "c")
         adj_product(0, 0)
         adj_product(0, 1)
+        interleave_grad(1, 0, on_v)
+        transpose_rows(1, "g")
+        adj_product(0, 2)
+        adj_product(0, 3)
+        build_cand(1)
+        copy_x(1, on_v)
+        interleave_grad(1, 1, on_s, 0, 8)
+        interleave_grad(1, 1, on_v, 8)
+        empty_transposed(1, "g")
+        transpose_rows(1, "c")
+        quantize_turned(1, "g")
 
-        for s in range(2, CHUNKS):
+        for s in range(2, CHUNKS - 1):
             old = s - 1
             if s + 2 < CHUNKS:
                 load_chunk(s + 2)
-            if s + 2 <= CHUNKS:
+            if s + 2 < CHUNKS - 1:
+                if s >= 3:
+                    store_state(s - 3)
+            elif s + 2 == CHUNKS - 1:
+                store_state(s - 3)
                 store_state(s - 2)
-            sigmoid(s)
+            empty_transposed(old, "c")
             quantize_grad(old, 0)
             quantize_grad(old, 1)
             state_product(old, 0)
             state_product(old, 1)
-            empty_transposed(old, "g")
-            interleave_grad(s, 0)
-            transpose_rows(old, "c")
-            adj_product(old - 1, 2)
-            adj_product(old - 1, 3)
-            compact_grad(s)
-            build_cand(s)
-            copy_x(s)
-            empty_transposed(old, "c")
-            gate_and_empty(old, 0)
-            gate_and_empty(old, 1)
-            state_product(old, 2)
-            state_product(old, 3)
-            transpose_rows(s, "g")
-            interleave_grad(s, 1)
-            quantize_turned(old, "g")
+            sigmoid(s)
+            interleave_grad(s, 0, on_v)
             quantize_turned(old, "c")
             adj_product(old, 0)
             adj_product(old, 1)
+            compact_grad(s)
+            gate_and_empty(old, 0)
+            state_product(old, 2)
+            gate_and_empty(old, 1)
+            transpose_rows(s, "g")
+            state_product(old, 3)
+            interleave_grad(s, 1, on_s, 0, 8)
+            build_cand(s)
+            copy_x(s, on_v)
+            empty_transposed(s, "g")
+            transpose_rows(s, "c")
+            adj_product(old, 2)
+            adj_product(old, 3)
+            interleave_grad(s, 1, on_s, 8)
             gate_and_empty(old, 2)
             gate_and_empty(old, 3)
-            if s + 2 >= CHUNKS:
+            if s + 2 >= CHUNKS - 1:
                 store_state(old)
+            quantize_turned(s, "g")
 
-        old = CHUNKS - 1
-        last = CHUNKS
-        empty_transposed(old, "g")
+        last = CHUNKS - 1
+        old = last - 1
+        empty_transposed(old, "c")
+        sigmoid(last)
         quantize_grad(old, 0)
         quantize_grad(old, 1)
-        transpose_rows(old, "c")
         state_product(old, 0)
         state_product(old, 1)
-        adj_product(old - 1, 2)
-        adj_product(old - 1, 3)
-        quantize_turned(old, "g")
-        empty_transposed(old, "c")
+        interleave_grad(last, 0, on_v)
+        interleave_grad(last, 1, on_s)
         gate_and_empty(old, 0)
-        gate_and_empty(old, 1)
-        transpose_rows(last, "g")
         state_product(old, 2)
+        gate_and_empty(old, 1)
         state_product(old, 3)
         quantize_turned(old, "c")
-        empty_transposed(last, "g")
+        for j in range(J):
+            adj_product(old, j)
         gate_and_empty(old, 2)
         gate_and_empty(old, 3)
         store_state(old)
+        compact_grad(last)
+        quantize_grad(last, 0)
+        quantize_grad(last, 1)
+        state_product(last, 0)
+        state_product(last, 1)
+        transpose_rows(last, "g")
+        build_cand(last)
+        copy_x(last, on_v)
+        empty_transposed(last, "g")
         transpose_rows(last, "c")
-        for j in range(J):
-            adj_product(old, j)
-        quantize_turned(last, "g")
+        gate_and_empty(last, 0)
+        gate_and_empty(last, 1)
+        store_state(last, 0, 2)
+        state_product(last, 2)
+        state_product(last, 3)
         empty_transposed(last, "c")
+        quantize_turned(last, "g")
+        gate_and_empty(last, 2)
         quantize_turned(last, "c")
-        out_rows = out_1.rearrange("(p j) n -> p j n", j=J)
+        gate_and_empty(last, 3)
+        store_state(last, 2, J)
         for j in range(J):
             adj_product(last, j)
         for j in range(J):
-            t = keep.tile([P, N], F32, name="dadj%d" % j)
-            dst = t[:].rearrange("p (r i) -> p r i", i=J)
-            src = acc[j][:].rearrange("p (i r) -> p r i", i=J)
-            if j % 2 == 0:
-                nc.scalar.copy(out=dst, in_=src)
-            else:
-                nc.vector.tensor_copy(out=dst, in_=src)
-            nc.sync.dma_start(out=out_rows[:, j, :], in_=t[:])
+            store_adj(j, (on_s, on_v)[j % 2])

@@ -26,7 +26,9 @@ KP = P * J
 WORDS = KP // 2
 CW = C // 2
 XW = DIN // 2
-SW = DOUT // 2
+LINES = C // DIN
+SLOTS = 36
+SHIFT = 4
 
 
 def entries(c):
@@ -116,7 +118,7 @@ def tile_agcrnlayer_pb_v_kernel(tc, adj, cheb2, x, state, r_logit, grad_out, out
         def quantize_adj(o):
             codes_a[o] = quantize(grouped[1][o], "a%d" % o, E4M3, keep)
 
-        def turn_x():
+        def turn_x(copy):
             words = x_rows[:].bitcast(F32)
             dst = x_nodes[:].bitcast(F32).rearrange("p b (h l w) -> p l b h w", h=2, l=2)
             for l in range(2):
@@ -124,7 +126,7 @@ def tile_agcrnlayer_pb_v_kernel(tc, adj, cheb2, x, state, r_logit, grad_out, out
                 for w in range(XW):
                     first = l * XW + w
                     nc.tensor.transpose(bank[:, w, :], words[:, first:first + (P - 1) * J * XW + 1:J * XW], ident[:])
-                nc.scalar.copy(out=dst[:, l], in_=bank[:].rearrange("p w (b h) -> p b h w", h=2))
+                copy(out=dst[:, l], in_=bank[:].rearrange("p w (b h) -> p b h w", h=2))
 
         def sigmoid(c, first=0, stop=None):
             stop = width(c) if stop is None else stop
@@ -141,41 +143,64 @@ def tile_agcrnlayer_pb_v_kernel(tc, adj, cheb2, x, state, r_logit, grad_out, out
         def quantize_grad(c, o):
             codes_g[c, o] = quantize(grouped[c % 2][o], "g%d" % o, E5M2, work)
 
-        def compact_grad(c):
-            t = work.tile([P, J, GROUP * C], BF16, name="rows_g", tag="rows_g")
-            dst = t[:].bitcast(F32)
-            src = raw[c, "grad"][:].bitcast(F32).rearrange("p b (j w) -> p b j w", j=J)
+        def line_runs(c, first):
+            runs = []
             if c == 0:
-                nc.scalar.copy(out=dst[:, :, 0:WORDS].rearrange("p j (b w) -> p b j w", b=GROUP), in_=src[:, :, :, XW:CW])
-                nc.scalar.copy(out=heads[:], in_=src[:, :, :, 0:XW])
+                for e in range(2):
+                    runs.append((slice(0, GROUP), slice(1 + e, LINES, 2), e, 4, 0))
+                return runs
+            for par in range(2):
+                for e in range(2):
+                    lo = first + (e - first) % 2
+                    line = LINES * par + lo
+                    runs.append((slice(par, GROUP - 1, 2), slice(lo, LINES, 2), line % 2, LINES, line // 2))
+            return runs
+
+        def plane(t, u):
+            shift = SHIFT * (1 - u)
+            return t[:, u, shift:shift + J * SLOTS, :].rearrange("p (j s) k -> p j s k", j=J)
+
+        def place(t, run):
+            bs, ls, u, pitch, start = run
+            nb = len(range(GROUP)[bs])
+            nl = len(range(LINES)[ls])
+            view = plane(t, u).rearrange("p j (b r) k -> p b j r k", r=pitch)
+            return view[:, 0:nb, :, start:start + nl, :]
+
+        def compact_grad(c):
+            t = work.tile([P, 2, J * SLOTS + SHIFT, DIN], BF16, name="rows_g", tag="rows_g")
+            words = t[:].bitcast(F32)
+            src = raw[c, "grad"][:].bitcast(F32).rearrange("p b (j l w) -> p b j l w", j=J, w=XW)
+            for run in line_runs(c, 0):
+                nc.scalar.copy(out=place(words, run), in_=src[:, run[0], :, run[1], :])
+            if c == 0:
+                nc.scalar.copy(out=heads[:], in_=src[:, :, :, 0, :])
             else:
-                dst = dst.rearrange("p j (b w) -> p b j w", b=GROUP)
-                nc.scalar.copy(out=dst[:, 0:GROUP - 1], in_=src[:, :, :, 0:CW])
-                nc.scalar.copy(out=dst[:, GROUP - 1, :, 0:XW], in_=heads[:, c - 1])
+                nc.scalar.copy(out=plane(words, 1)[:, :, 31, :], in_=heads[:, c - 1])
             rows[c, "g"] = t
 
         def build_cand(c):
-            t = work.tile([P, J, GROUP * C], BF16, name="rows_c", tag="rows_c")
-            if c == 0:
-                dst = t[:, :, 0:KP].rearrange("p j (b c) -> p b j c", b=GROUP)
-            else:
-                dst = t[:].rearrange("p j (b c) -> p b j c", b=GROUP)[:, 0:GROUP - 1, :, DIN:C]
-            nc.vector.tensor_tensor(out=dst, in0=gate[c][:].rearrange("p b (j c) -> p b j c", j=J),
-                                    in1=raw[c, "state"][:].rearrange("p b (j c) -> p b j c", j=J), op=MULT)
+            t = work.tile([P, 2, J * SLOTS + SHIFT, DIN], BF16, name="rows_c", tag="rows_c")
+            r = gate[c][:].rearrange("p b (j l k) -> p b j l k", j=J, k=DIN)
+            s = raw[c, "state"][:].rearrange("p b (j l k) -> p b j l k", j=J, k=DIN)
+            for run in line_runs(c, 1):
+                ls = slice(run[1].start - 1, LINES - 1, 2)
+                nc.vector.tensor_tensor(out=place(t[:], run), in0=r[:, run[0], :, ls, :], in1=s[:, run[0], :, ls, :], op=MULT)
             rows[c, "c"] = t
 
         def copy_x(c, copy):
-            view = rows[c, "c"][:].rearrange("p j (b c) -> p b j c", b=GROUP)
-            copy(out=view[:, :, :, 0:DIN],
-                 in_=x_nodes[:, (c - 1) * GROUP:c * GROUP, :].rearrange("p b (j c) -> p b j c", j=J))
+            src = x_nodes[:, (c - 1) * GROUP:c * GROUP, :].rearrange("p (b u) (j k) -> p u j b k", u=2, j=J)
+            dst = rows[c, "c"][:, :, SHIFT:, :].rearrange("p u (j b r) k -> p u j b r k", j=J, r=LINES)
+            copy(out=dst[:, :, :, :, 0, :], in_=src)
 
         def transpose_rows(g, which, halves=(0, 1)):
             words = rows[g, which][:].bitcast(F32)
+            planes = [plane(words, u).rearrange("p j s w -> p j (s w)") for u in range(2)]
             for h in halves:
                 bank = ps_rot.tile([P, 2, 2, P], F32, name="bank_t", tag="bank_t")
                 for jj in range(2):
                     for u in range(2):
-                        nc.tensor.transpose(bank[:, jj, u, :], words[:, 2 * h + jj, u:WORDS:2], ident[:])
+                        nc.tensor.transpose(bank[:, jj, u, :], planes[u][:, 2 * h + jj, 0:P], ident[:])
                 turned[g, which, h] = bank
 
         def empty_transposed(g, which, copies=(on_s, on_s)):
@@ -260,7 +285,7 @@ def tile_agcrnlayer_pb_v_kernel(tc, adj, cheb2, x, state, r_logit, grad_out, out
         quantize_turned(0, "g")
         empty_transposed(0, "c")
         compact_grad(1)
-        turn_x()
+        turn_x(on_s)
         gate_and_empty(0, 2)
         gate_and_empty(0, 3)
         quantize_turned(0, "c")
@@ -268,14 +293,14 @@ def tile_agcrnlayer_pb_v_kernel(tc, adj, cheb2, x, state, r_logit, grad_out, out
         adj_product(0, 1)
         interleave_grad(1, 0, on_v)
         transpose_rows(1, "g")
-        adj_product(0, 2)
-        adj_product(0, 3)
         build_cand(1)
         copy_x(1, on_v)
         interleave_grad(1, 1, on_s, 0, 8)
         interleave_grad(1, 1, on_v, 8)
         empty_transposed(1, "g")
         transpose_rows(1, "c")
+        adj_product(0, 2)
+        adj_product(0, 3)
         quantize_turned(1, "g")
 
         for s in range(2, CHUNKS - 1):
@@ -341,9 +366,9 @@ def tile_agcrnlayer_pb_v_kernel(tc, adj, cheb2, x, state, r_logit, grad_out, out
         compact_grad(last)
         quantize_grad(last, 0)
         quantize_grad(last, 1)
+        transpose_rows(last, "g")
         state_product(last, 0)
         state_product(last, 1)
-        transpose_rows(last, "g")
         build_cand(last)
         copy_x(last, on_v)
         empty_transposed(last, "g")

from contextlib import ExitStack

import concourse.mybir as mybir
from concourse.masks import make_identity

N, DIN, DOUT, B = 512, 8, 64, 64
C = DIN + DOUT

FLOPS = 2 * (2 * N) * N * (B * DOUT) + 2 * N * N * (B * C)
BYTES = 2 * (2 * N * N + B * N * DIN + 2 * B * N * DOUT + B * N * (C + DOUT)) + 4 * (B * N * DOUT + N * N)

F32 = mybir.dt.float32
BF16 = mybir.dt.bfloat16
U32 = mybir.dt.uint32
U8 = mybir.dt.uint8
E4M3 = mybir.dt.float8_e4m3fn_x4
E5M2 = mybir.dt.float8_e5m2_x4
SIGMOID = mybir.ActivationFunctionType.Sigmoid
MULT = mybir.AluOpType.mult

P = 128
J = 4
GROUP = 8
CHUNKS = B // GROUP + 1
KP = P * J
WORDS = KP // 2
CW = C // 2
XW = DIN // 2
LINES = C // DIN
SLOTS = 36
SHIFT = 4


def entries(c):
    if c == 0:
        return slice(GROUP - 1, B, GROUP)
    return slice((c - 1) * GROUP, c * GROUP - 1)


def width(c):
    return GROUP if c == 0 else GROUP - 1


def tile_agcrnlayer_pb_v_kernel(tc, adj, cheb2, x, state, r_logit, grad_out, out_0, out_1):
    nc = tc.nc
    with ExitStack() as ctx:
        keep = ctx.enter_context(tc.tile_pool(name="keep", bufs=1))
        load = ctx.enter_context(tc.tile_pool(name="load", bufs=3))
        work = ctx.enter_context(tc.tile_pool(name="work", bufs=2))
        outp = ctx.enter_context(tc.tile_pool(name="outp", bufs=4))
        ps_acc = ctx.enter_context(tc.psum_pool(name="ps_acc", bufs=1))
        ps_rot = ctx.enter_context(tc.psum_pool(name="ps_rot", bufs=2))
        ctx.enter_context(tc.manual_schedule())

        on_v = nc.vector.tensor_copy
        on_s = nc.scalar.copy

        ident = keep.tile([P, P], F32, name="ident")
        make_identity(nc, ident[:])

        acc = [ps_acc.tile([P, N], F32, name="acc%d" % j, tag="acc%d" % j) for j in range(J)]
        grouped = [[keep.tile([P, KP * J], BF16, name="gil%d%d" % (i, o), align_bytes=64) for o in range(2)] for i in range(2)]
        x_rows = keep.tile([P, N * DIN], BF16, name="x_rows")
        x_nodes = keep.tile([P, B, J * DIN], BF16, name="x_nodes")
        heads = keep.tile([P, GROUP, J, XW], F32, name="heads")

        raw = {}
        codes_a = {}
        gate = {}
        codes_g = {}
        rows = {}
        turned = {}
        codes_t = {}
        sums = {}
        result = {}

        def load_logit(c, first=0, stop=None):
            stop = width(c) if stop is None else stop
            t = load.tile([P, stop - first, J * DOUT], BF16, name="logit", tag="logit")
            src = r_logit[entries(c)][first:stop]
            nc.sync.dma_start(out=t[:], in_=src.rearrange("b (p j) c -> p b (j c)", j=J))
            raw[c, "logit", first] = t

        def load_grad(c):
            t = load.tile([P, width(c), J * 2 * C], BF16, name="grad", tag="grad")
            nc.sync.dma_start(out=t[:], in_=grad_out[entries(c)].rearrange("b (p j) o c -> p b (j o c)", j=J))
            raw[c, "grad"] = t

        def load_state(c):
            t = load.tile([P, width(c), J * DOUT], BF16, name="stat", tag="stat")
            nc.sync.dma_start(out=t[:], in_=state[entries(c)].rearrange("b (p j) c -> p b (j c)", j=J))
            raw[c, "state"] = t

        def load_chunk(c):
            load_logit(c)
            load_grad(c)
            load_state(c)

        def load_adj(o):
            t = keep.tile([P, J, N], BF16, name="a_raw%d" % o)
            nc.sync.dma_start(out=t[:], in_=(adj, cheb2)[o].rearrange("(p j) n -> p j n", j=J))
            raw["a", o] = t

        def load_x(h):
            skip = 2 * h * DIN
            nc.sync.dma_start(out=x_rows[h:P:2, 0:N * DIN - skip], in_=x.rearrange("b n c -> b (n c)")[:, skip:N * DIN])

        def quantize(src, name, fmt, pool):
            codes = pool.tile([P, KP], U32, name=name + "_codes", tag=name + "_codes", align_bytes=64)
            scales = pool.tile([P, KP], U8, name=name + "_scales", tag=name + "_scales", align_bytes=64)
            nc.vector.quantize_mx(out=codes[:].bitcast(fmt), scales=scales[:], in_=src[:])
            return codes, scales

        def interleave_adj(o):
            nc.vector.tensor_copy(out=grouped[1][o][:].rearrange("p (t m j) -> p t m j", t=J, j=J),
                                  in_=raw["a", o][:].rearrange("p j (m t) -> p t m j", t=J))

        def quantize_adj(o):
            codes_a[o] = quantize(grouped[1][o], "a%d" % o, E4M3, keep)

        def turn_x(copy):
            words = x_rows[:].bitcast(F32)
            dst = x_nodes[:].bitcast(F32).rearrange("p b (h l w) -> p l b h w", h=2, l=2)
            for l in range(2):
                bank = ps_rot.tile([P, XW, P], F32, name="bank_t", tag="bank_t")
                for w in range(XW):
                    first = l * XW + w
                    nc.tensor.transpose(bank[:, w, :], words[:, first:first + (P - 1) * J * XW + 1:J * XW], ident[:])
                copy(out=dst[:, l], in_=bank[:].rearrange("p w (b h) -> p b h w", h=2))

        def sigmoid(c, first=0, stop=None):
            stop = width(c) if stop is None else stop
            if first == 0:
                gate[c] = load.tile([P, width(c), J * DOUT], F32, name="gate", tag="gate")
            nc.scalar.activation(out=gate[c][:, first:stop, :], in_=raw[c, "logit", first][:], func=SIGMOID)

        def interleave_grad(c, o, copy, first=0, stop=16):
            src = raw[c, "grad"][:].rearrange("p b (j o c) -> p b j o c", j=J, o=2)[:, :, :, o, DIN:C]
            src = src.rearrange("p b j (q i) -> p q b j i", i=4)
            dst = grouped[c % 2][o][:].rearrange("p (b q i j) -> p q b j i", b=GROUP, i=4, j=J)
            copy(out=dst[:, first:stop, 0:width(c)], in_=src[:, first:stop])

        def quantize_grad(c, o):
            codes_g[c, o] = quantize(grouped[c % 2][o], "g%d" % o, E5M2, work)

        def line_runs(c, first):
            runs = []
            if c == 0:
                for e in range(2):
                    runs.append((slice(0, GROUP), slice(1 + e, LINES, 2), e, 4, 0))
                return runs
            for par in range(2):
                for e in range(2):
                    lo = first + (e - first) % 2
                    line = LINES * par + lo
                    runs.append((slice(par, GROUP - 1, 2), slice(lo, LINES, 2), line % 2, LINES, line // 2))
            return runs

        def plane(t, u):
            shift = SHIFT * (1 - u)
            return t[:, u, shift:shift + J * SLOTS, :].rearrange("p (j s) k -> p j s k", j=J)

        def place(t, run):
            bs, ls, u, pitch, start = run
            nb = len(range(GROUP)[bs])
            nl = len(range(LINES)[ls])
            view = plane(t, u).rearrange("p j (b r) k -> p b j r k", r=pitch)
            return view[:, 0:nb, :, start:start + nl, :]

        def compact_grad(c):
            t = work.tile([P, 2, J * SLOTS + SHIFT, DIN], BF16, name="rows_g", tag="rows_g")
            words = t[:].bitcast(F32)
            src = raw[c, "grad"][:].bitcast(F32).rearrange("p b (j l w) -> p b j l w", j=J, w=XW)
            for run in line_runs(c, 0):
                nc.scalar.copy(out=place(words, run), in_=src[:, run[0], :, run[1], :])
            if c == 0:
                nc.scalar.copy(out=heads[:], in_=src[:, :, :, 0, :])
            else:
                nc.scalar.copy(out=plane(words, 1)[:, :, 31, :], in_=heads[:, c - 1])
            rows[c, "g"] = t

        def build_cand(c):
            t = work.tile([P, 2, J * SLOTS + SHIFT, DIN], BF16, name="rows_c", tag="rows_c")
            r = gate[c][:].rearrange("p b (j l k) -> p b j l k", j=J, k=DIN)
            s = raw[c, "state"][:].rearrange("p b (j l k) -> p b j l k", j=J, k=DIN)
            for run in line_runs(c, 1):
                ls = slice(run[1].start - 1, LINES - 1, 2)
                nc.vector.tensor_tensor(out=place(t[:], run), in0=r[:, run[0], :, ls, :], in1=s[:, run[0], :, ls, :], op=MULT)
            rows[c, "c"] = t

        def copy_x(c, copy):
            src = x_nodes[:, (c - 1) * GROUP:c * GROUP, :].rearrange("p (b u) (j k) -> p u j b k", u=2, j=J)
            dst = rows[c, "c"][:, :, SHIFT:, :].rearrange("p u (j b r) k -> p u j b r k", j=J, r=LINES)
            copy(out=dst[:, :, :, :, 0, :], in_=src)

        def transpose_rows(g, which, halves=(0, 1)):
            words = rows[g, which][:].bitcast(F32)
            planes = [plane(words, u).rearrange("p j s w -> p j (s w)") for u in range(2)]
            for h in halves:
                bank = ps_rot.tile([P, 2, 2, P], F32, name="bank_t", tag="bank_t")
                for jj in range(2):
                    for u in range(2):
                        nc.tensor.transpose(bank[:, jj, u, :], planes[u][:, 2 * h + jj, 0:P], ident[:])
                turned[g, which, h] = bank

        def empty_transposed(g, which, copies=(on_s, on_s)):
            t = work.tile([P, N * J], BF16, name="turned_" + which, tag="turned_" + which, align_bytes=64)
            view = t[:].bitcast(F32).rearrange("q (j r u) -> q j r u", j=J, u=2)
            for h in range(2):
                copies[h](out=view[:, 2 * h:2 * h + 2], in_=turned[g, which, h][:].rearrange("q j u r -> q j r u"))
            turned[g, which] = t

        def quantize_turned(g, which):
            codes_t[g, which] = quantize(turned[g, which], "t" + which, E5M2 if which == "g" else E4M3, work)

        def state_product(c, t):
            bank = ps_rot.tile([P, KP], F32, name="bank_s", tag="bank_s")
            cols = slice(t * P, (t + 1) * P)
            for o in range(2):
                a_codes, a_scales = codes_a[o]
                g_codes, g_scales = codes_g[c, o]
                nc.tensor.matmul_mx(out=bank[:], lhsT=a_codes[:, cols].bitcast(E4M3), lhsT_scale=a_scales[:, cols],
                                    rhs=g_codes[:].bitcast(E5M2), rhs_scale=g_scales[:], start=(o == 0), stop=(o == 1))
            sums[c, t] = bank

        def gate_and_empty(c, t):
            if t == 0:
                result[c] = outp.tile([P, width(c), J * DOUT], F32, name="dstate", tag="dstate")
            cols = slice(t * DOUT, (t + 1) * DOUT)
            src = sums[c, t][:].rearrange("p (b c) -> p b c", b=GROUP)[:, 0:width(c)]
            nc.vector.tensor_tensor(out=result[c][:, :, cols], in0=src, in1=gate[c][:, :, cols], op=MULT)

        def store_state(c, first=0, stop=J):
            cols = slice(first * DOUT, stop * DOUT)
            dst = out_0[entries(c)].rearrange("b (p j) c -> p b (j c)", j=J)
            nc.sync.dma_start(out=dst[:, :, cols], in_=result[c][:, :, cols])

        def adj_product(g, j):
            g_codes, g_scales = codes_t[g, "g"]
            c_codes, c_scales = codes_t[g, "c"]
            cols = slice(j * P, (j + 1) * P)
            nc.tensor.matmul_mx(out=acc[j][:], lhsT=g_codes[:, cols].bitcast(E5M2), lhsT_scale=g_scales[:, cols],
                                rhs=c_codes[:].bitcast(E4M3), rhs_scale=c_scales[:], start=(g == 0), stop=(g == CHUNKS - 1))

        def store_adj(j, copy):
            t = keep.tile([P, N], F32, name="dadj%d" % j)
            copy(out=t[:].rearrange("p (r i) -> p r i", i=J), in_=acc[j][:].rearrange("p (i r) -> p r i", i=J))
            nc.sync.dma_start(out=out_1.rearrange("(p j) n -> p j n", j=J)[:, j, :], in_=t[:])

        load_logit(0, 0, 1)
        load_adj(0)
        load_adj(1)
        load_grad(0)
        load_logit(0, 1)
        load_state(0)
        load_x(0)
        load_logit(1)
        load_x(1)
        load_grad(1)
        load_state(1)
        sigmoid(0, 0, 1)
        load_chunk(2)
        interleave_adj(0)
        interleave_adj(1)
        quantize_adj(0)
        quantize_adj(1)
        compact_grad(0)
        interleave_grad(0, 0, on_v)
        interleave_grad(0, 1, on_v)
        transpose_rows(0, "g")
        sigmoid(0, 1)
        quantize_grad(0, 0)
        quantize_grad(0, 1)
        state_product(0, 0)
        state_product(0, 1)
        empty_transposed(0, "g")
        build_cand(0)
        transpose_rows(0, "c")
        load_chunk(3)
        sigmoid(1)
        gate_and_empty(0, 0)
        gate_and_empty(0, 1)
        state_product(0, 2)
        state_product(0, 3)
        quantize_turned(0, "g")
        empty_transposed(0, "c")
        compact_grad(1)
        turn_x(on_s)
        gate_and_empty(0, 2)
        gate_and_empty(0, 3)
        quantize_turned(0, "c")
        adj_product(0, 0)
        adj_product(0, 1)
        interleave_grad(1, 0, on_v)
        transpose_rows(1, "g")
        build_cand(1)
        copy_x(1, on_v)
        interleave_grad(1, 1, on_s, 0, 8)
        interleave_grad(1, 1, on_v, 8)
        empty_transposed(1, "g")
        transpose_rows(1, "c")
        adj_product(0, 2)
        adj_product(0, 3)
        quantize_turned(1, "g")

        for s in range(2, CHUNKS - 1):
            old = s - 1
            if s + 2 < CHUNKS:
                load_chunk(s + 2)
            if s + 2 < CHUNKS - 1:
                if s >= 3:
                    store_state(s - 3)
            elif s + 2 == CHUNKS - 1:
                store_state(s - 3)
                store_state(s - 2)
            empty_transposed(old, "c")
            quantize_grad(old, 0)
            quantize_grad(old, 1)
            state_product(old, 0)
            state_product(old, 1)
            sigmoid(s)
            interleave_grad(s, 0, on_v)
            quantize_turned(old, "c")
            adj_product(old, 0)
            adj_product(old, 1)
            compact_grad(s)
            gate_and_empty(old, 0)
            state_product(old, 2)
            gate_and_empty(old, 1)
            transpose_rows(s, "g")
            state_product(old, 3)
            interleave_grad(s, 1, on_s, 0, 8)
            build_cand(s)
            copy_x(s, on_v)
            empty_transposed(s, "g")
            transpose_rows(s, "c")
            adj_product(old, 2)
            adj_product(old, 3)
            interleave_grad(s, 1, on_s, 8)
            gate_and_empty(old, 2)
            gate_and_empty(old, 3)
            if s + 2 >= CHUNKS - 1:
                store_state(old)
            quantize_turned(s, "g")

        last = CHUNKS - 1
        old = last - 1
        empty_transposed(old, "c")
        sigmoid(last)
        quantize_grad(old, 0)
        quantize_grad(old, 1)
        state_product(old, 0)
        state_product(old, 1)
        interleave_grad(last, 0, on_v)
        interleave_grad(last, 1, on_s)
        gate_and_empty(old, 0)
        state_product(old, 2)
        gate_and_empty(old, 1)
        state_product(old, 3)
        quantize_turned(old, "c")
        for j in range(J):
            adj_product(old, j)
        gate_and_empty(old, 2)
        gate_and_empty(old, 3)
        store_state(old)
        compact_grad(last)
        quantize_grad(last, 0)
        quantize_grad(last, 1)
        transpose_rows(last, "g")
        state_product(last, 0)
        state_product(last, 1)
        build_cand(last)
        copy_x(last, on_v)
        empty_transposed(last, "g")
        transpose_rows(last, "c")
        gate_and_empty(last, 0)
        gate_and_empty(last, 1)
        store_state(last, 0, 2)
        state_product(last, 2)
        state_product(last, 3)
        empty_transposed(last, "c")
        quantize_turned(last, "g")
        gate_and_empty(last, 2)
        quantize_turned(last, "c")
        gate_and_empty(last, 3)
        store_state(last, 2, J)
        for j in range(J):
            adj_product(last, j)
        for j in range(J):
            store_adj(j, (on_s, on_v)[j % 2])
